import numpy as np
import ml_dtypes


def mxq(x, axis, fmt="e4m3"):
    dtype, down = {"e4m3": (ml_dtypes.float8_e4m3fn, 7), "e5m2": (ml_dtypes.float8_e5m2, 14)}[fmt]
    v = np.moveaxis(np.asarray(x, np.float32).astype(ml_dtypes.bfloat16).astype(np.float64), axis, -1)
    blocks = v.reshape(v.shape[:-1] + (-1, 32))
    amax = np.abs(blocks).max(-1, keepdims=True)
    byte = np.maximum(np.where(amax > 0, np.frexp(amax)[1] - 1 + 127, 0) - down, 1)
    scale = np.exp2(byte - 127.0)
    codes = (blocks / scale).astype(np.float32).astype(dtype).astype(np.float64)
    return np.moveaxis((codes * scale).reshape(v.shape), -1, axis)


WIDE = False


def mx_kscale(k):
    if not WIDE:
        return np.ones(k)
    levels = np.array([10, -10, 5, -5, 0])
    a = np.random.permutation(np.resize(levels, k // 512 * 4)).reshape(k // 512, 4)
    idx = np.arange(k)
    return np.exp2(a[idx // 512, idx % 128 // 32])


BF16 = ml_dtypes.bfloat16


def bf(x):
    return np.asarray(x, np.float32).astype(BF16)


def f64(x):
    return np.asarray(x).astype(np.float64)


B, IN, H = 512, 1024, 1024


def sigmoid(v):
    return 1.0 / (1.0 + np.exp(-v))


def setup_inputs():
    s, t = mx_kscale(IN), mx_kscale(H)
    a = np.sqrt(2.0 / (IN + H))
    return {
        "x": bf(np.random.standard_normal((B, IN)) * s),
        "h_prev": bf(np.random.standard_normal((B, H)) * t),
        "m_prev": bf(np.random.standard_normal((B, H)) * 0.5),
        "Wi_x": bf(np.random.standard_normal((H, IN)) * a / s),
        "b_i": bf(np.random.standard_normal(H) * 0.3),
        "Wi_h": bf(np.random.standard_normal((H, H)) * a / t),
        "Wf_x": bf(np.random.standard_normal((H, IN)) * a / s),
        "b_f": bf(2.0 + np.random.standard_normal(H) * 0.3),
        "Wf_h": bf(np.random.standard_normal((H, H)) * a / t),
    }


def reference(x, h_prev, m_prev, Wi_x, b_i, Wi_h, Wf_x, b_f, Wf_h):
    xq = mxq(f64(x), 1, "e4m3")
    hq = mxq(f64(h_prev), 1, "e4m3")
    i_tilde = (xq @ mxq(f64(Wi_x), 1, "e4m3").T) + f64(b_i) + (hq @ mxq(f64(Wi_h), 1, "e4m3").T)
    f_aff = (xq @ mxq(f64(Wf_x), 1, "e4m3").T) + f64(b_f) + (hq @ mxq(f64(Wf_h), 1, "e4m3").T)
    log_f = np.log(np.maximum(sigmoid(f_aff), 1e-8))
    m_t = np.maximum(log_f + f64(m_prev), i_tilde)
    i_prime = np.exp(i_tilde - m_t)
    f_prime = np.exp(log_f + f64(m_prev) - m_t)
    return m_t, i_prime, f_prime

@@ -1,0 +1,242 @@
+from contextlib import ExitStack
+
+import concourse.mybir as mybir
+from concourse.masks import make_identity
+
+F32 = mybir.dt.float32
+BF16 = mybir.dt.bfloat16
+U32 = mybir.dt.uint32
+U8 = mybir.dt.uint8
+FP8X4 = mybir.dt.float8_e4m3fn_x4
+ACT = mybir.ActivationFunctionType
+ALU = mybir.AluOpType
+
+P = 128
+BATCH = 512
+SIDE_K = 1024
+HIDDEN = 1024
+K_PASS = 512
+SIDES = 2
+SIDE_PASSES = SIDE_K // K_PASS
+PASSES = SIDES * SIDE_PASSES
+BLOCK_ROWS = 256
+ROW_TILES = BLOCK_ROWS // P
+BATCH_TILES = BATCH // P
+CHUNKS = HIDDEN // BLOCK_ROWS
+SIDE_WORDS = SIDE_K // 2
+WORD_TILES = SIDE_WORDS // P
+SIGMOID_FLOOR = 1e-8
+
+FLOPS = 2 * BATCH * (SIDES * SIDE_K) * (2 * HIDDEN)
+
+
+def tile_slstmlayer_pa_kernel(
+    tc, x, h_prev, m_prev, Wi_x, b_i, Wi_h, Wf_x, b_f, Wf_h, out_0, out_1, out_2
+):
+    nc = tc.nc
+    with ExitStack() as ctx:
+        const = ctx.enter_context(tc.tile_pool(name="const", bufs=1))
+        raw_pool = ctx.enter_context(tc.tile_pool(name="raw", bufs=1))
+        grouped_pool = ctx.enter_context(tc.tile_pool(name="grouped", bufs=4))
+        act_pool = ctx.enter_context(tc.tile_pool(name="act_codes", bufs=1))
+        w_pool = ctx.enter_context(tc.tile_pool(name="w_codes", bufs=3))
+        keep = ctx.enter_context(tc.tile_pool(name="keep", bufs=1))
+        work = ctx.enter_context(tc.tile_pool(name="work", bufs=3))
+        t_psum = ctx.enter_context(tc.psum_pool(name="t_psum", bufs=4))
+        acc_psum = ctx.enter_context(tc.psum_pool(name="acc_psum", bufs=4))
+
+        ident = const.tile([P, P], F32, name="ident")
+        make_identity(nc, ident[:])
+
+        def by_batch(ap):
+            return ap.rearrange("(p t) n -> p t n", t=BATCH_TILES)
+
+        blocks = []
+        for pair in range(BATCH_TILES // ROW_TILES):
+            tiles = slice(pair * ROW_TILES, (pair + 1) * ROW_TILES)
+            blocks.append((by_batch(x)[:, tiles, :], by_batch(h_prev)[:, tiles, :]))
+        for w_x, w_h in ((Wf_x, Wf_h), (Wi_x, Wi_h)):
+            for c in range(CHUNKS):
+                rows = slice(c * BLOCK_ROWS, (c + 1) * BLOCK_ROWS)
+                blocks.append(
+                    (
+                        w_x[rows, :].rearrange("(t p) k -> p t k", p=P),
+                        w_h[rows, :].rearrange("(t p) k -> p t k", p=P),
+                    )
+                )
+        ACT_BLOCKS = BATCH_TILES // ROW_TILES
+        UNITS = 2 * CHUNKS
+
+        raw = []
+
+        def load_block(k):
+            sides = []
+            for s in range(SIDES):
+                t = raw_pool.tile([P, ROW_TILES * SIDE_K], BF16, name="raw_%d_%d" % (k, s))
+                nc.sync.dma_start(
+                    out=t[:].rearrange("p (t k) -> p t k", t=ROW_TILES), in_=blocks[k][s]
+                )
+                sides.append(t)
+            raw.append(sides)
+
+        bias_f = const.tile([P, HIDDEN], BF16, name="bias_f")
+        bias_i = const.tile([P, HIDDEN], BF16, name="bias_i")
+        m_raw = const.tile([P, BATCH_TILES, HIDDEN], BF16, name="m_raw")
+        for k in range(ACT_BLOCKS + 2):
+            load_block(k)
+        nc.sync.dma_start(out=bias_f[:], in_=b_f.partition_broadcast(P))
+        for k in range(ACT_BLOCKS + 2, ACT_BLOCKS + CHUNKS + 1):
+            load_block(k)
+        nc.sync.dma_start(out=m_raw[:], in_=by_batch(m_prev))
+        nc.sync.dma_start(out=bias_i[:], in_=b_i.partition_broadcast(P))
+        for k in range(ACT_BLOCKS + CHUNKS + 1, ACT_BLOCKS + UNITS):
+            load_block(k)
+
+        grouped = {}
+        codes = {}
+        scales = {}
+
+        def transpose_block(k):
+            for s in range(SIDES):
+                words = raw[k][s][:].bitcast(F32)
+                g = grouped_pool.tile(
+                    [P, SIDE_PASSES * BLOCK_ROWS * 4], BF16, name="grouped", align_bytes=64
+                )
+                g_words = g[:].bitcast(F32).rearrange(
+                    "p (g c u) -> p g c u", g=SIDE_PASSES, u=2
+                )
+                for t in range(ROW_TILES):
+                    bank = t_psum.tile([P, WORD_TILES, P], F32, name="bank")
+                    for j in range(WORD_TILES):
+                        first = t * SIDE_WORDS + j * P
+                        nc.tensor.transpose(bank[:, j, :], words[:, first : first + P], ident[:])
+                    nc.scalar.copy(
+                        out=g_words[:, :, t * P : (t + 1) * P, :],
+                        in_=bank[:].rearrange("p (g u) r -> p g r u", u=2),
+                    )
+                grouped[(k, s)] = g
+
+        def quantise_block(k):
+            pool = act_pool if k < ACT_BLOCKS else w_pool
+            tag = "act_%d" % k if k < ACT_BLOCKS else "w"
+            cd = pool.tile(
+                [P, PASSES * BLOCK_ROWS], U32, name="codes_" + tag, align_bytes=64
+            )
+            sc = pool.tile(
+                [P, PASSES * BLOCK_ROWS], U8, name="scales_" + tag, align_bytes=64
+            )
+            for s in range(SIDES):
+                cols = slice(s * SIDE_PASSES * BLOCK_ROWS, (s + 1) * SIDE_PASSES * BLOCK_ROWS)
+                nc.vector.quantize_mx(
+                    out=cd[:, cols].bitcast(FP8X4), scales=sc[:, cols], in_=grouped[(k, s)][:]
+                )
+            codes[k] = cd
+            scales[k] = sc
+
+        acc = {}
+
+        def multiply(u):
+            k = ACT_BLOCKS + u
+            for pair in range(ACT_BLOCKS):
+                bank = acc_psum.tile([P, ROW_TILES, BLOCK_ROWS], F32, name="acc")
+                for t in range(ROW_TILES):
+                    for q in range(PASSES):
+                        a_cols = slice(q * BLOCK_ROWS + t * P, q * BLOCK_ROWS + (t + 1) * P)
+                        w_cols = slice(q * BLOCK_ROWS, (q + 1) * BLOCK_ROWS)
+                        nc.tensor.matmul_mx(
+                            out=bank[:, t, :],
+                            lhsT=codes[pair][:, a_cols].bitcast(FP8X4),
+                            lhsT_scale=scales[pair][:, a_cols],
+                            rhs=codes[k][:, w_cols].bitcast(FP8X4),
+                            rhs_scale=scales[k][:, w_cols],
+                            start=(q == 0),
+                            stop=(q == PASSES - 1),
+                        )
+                acc[(u, pair)] = bank
+
+        pre = {}
+
+        def add_bias(u):
+            bias = bias_f if u < CHUNKS else bias_i
+            c = u % CHUNKS
+            feats = slice(c * BLOCK_ROWS, (c + 1) * BLOCK_ROWS)
+            out = work.tile([P, BATCH_TILES, BLOCK_ROWS], F32, name="pre")
+            for pair in range(ACT_BLOCKS):
+                nc.vector.tensor_tensor(
+                    out=out[:, pair * ROW_TILES : (pair + 1) * ROW_TILES, :],
+                    in0=acc[(u, pair)][:],
+                    in1=bias[:, feats].unsqueeze(1).to_broadcast([P, ROW_TILES, BLOCK_ROWS]),
+                    op=ALU.add,
+                )
+            pre[u] = out
+
+        decay = {}
+
+        def sigmoid(c):
+            t = keep.tile([P, BATCH_TILES, BLOCK_ROWS], F32, name="decay_%d" % c)
+            nc.scalar.activation(out=t[:], in_=pre[c][:], func=ACT.Sigmoid)
+            decay[c] = t
+
+        def clamp(c):
+            t = decay[c]
+            nc.vector.tensor_scalar_max(out=t[:], in0=t[:], scalar1=SIGMOID_FLOOR)
+
+        def log(c):
+            t = decay[c]
+            nc.scalar.activation(out=t[:], in_=t[:], func=ACT.Ln)
+
+        def add_m_prev(c):
+            feats = slice(c * BLOCK_ROWS, (c + 1) * BLOCK_ROWS)
+            t = decay[c]
+            nc.vector.tensor_tensor(out=t[:], in0=t[:], in1=m_raw[:, :, feats], op=ALU.add)
+
+        exps = {}
+
+        def stabilise_stage(c):
+            feats = slice(c * BLOCK_ROWS, (c + 1) * BLOCK_ROWS)
+            i_tilde = pre[CHUNKS + c]
+            a = decay[c]
+            m_t = work.tile([P, BATCH_TILES, BLOCK_ROWS], F32, name="m_t")
+            nc.vector.tensor_tensor(out=m_t[:], in0=a[:], in1=i_tilde[:], op=ALU.max)
+            nc.sync.dma_start(out=by_batch(out_0)[:, :, feats], in_=m_t[:])
+            nc.vector.tensor_tensor(out=i_tilde[:], in0=i_tilde[:], in1=a[:], op=ALU.subtract)
+            i_p = work.tile([P, BATCH_TILES, BLOCK_ROWS], F32, name="i_p")
+            f_p = work.tile([P, BATCH_TILES, BLOCK_ROWS], F32, name="f_p")
+            nc.vector.tensor_scalar_min(out=i_p[:], in0=i_tilde[:], scalar1=0.0)
+            nc.vector.tensor_scalar(
+                out=f_p[:], in0=i_tilde[:], scalar1=-1.0, scalar2=0.0, op0=ALU.mult, op1=ALU.min
+            )
+            exps[c] = (i_p, f_p)
+
+        def exp_stage(c):
+            feats = slice(c * BLOCK_ROWS, (c + 1) * BLOCK_ROWS)
+            for t, out in zip(exps[c], (out_1, out_2)):
+                nc.scalar.activation(out=t[:], in_=t[:], func=ACT.Exp)
+                nc.sync.dma_start(out=by_batch(out)[:, :, feats], in_=t[:])
+
+        ctx.enter_context(tc.manual_schedule())
+        for k in range(ACT_BLOCKS + 1):
+            transpose_block(k)
+            quantise_block(k)
+        for u in range(UNITS + 2):
+            logs = [2 * (u - CHUNKS - 1) + i for i in range(2)] if u in (CHUNKS + 1, CHUNKS + 2) else []
+            for c in logs:
+                log(c)
+            if u + 1 < UNITS:
+                transpose_block(ACT_BLOCKS + u + 1)
+            if u < UNITS:
+                multiply(u)
+            if 1 <= u <= UNITS:
+                add_bias(u - 1)
+            if 2 <= u <= CHUNKS + 1:
+                clamp(u - 2)
+            for c in logs:
+                add_m_prev(c)
+            if u + 1 < UNITS:
+                quantise_block(ACT_BLOCKS + u + 1)
+            if 1 <= u <= CHUNKS:
+                sigmoid(u - 1)
+            if CHUNKS + 1 <= u <= UNITS:
+                stabilise_stage(u - 1 - CHUNKS)
+            if CHUNKS + 2 <= u:
+                exp_stage(u - 2 - CHUNKS)

@@ -197,15 +197,23 @@ def tile_slstmlayer_pa_kernel(
             i_tilde = pre[CHUNKS + c]
             a = decay[c]
             m_t = work.tile([P, BATCH_TILES, BLOCK_ROWS], F32, name="m_t")
-            nc.vector.tensor_tensor(out=m_t[:], in0=a[:], in1=i_tilde[:], op=ALU.max)
-            nc.sync.dma_start(out=by_batch(out_0)[:, :, feats], in_=m_t[:])
-            nc.vector.tensor_tensor(out=i_tilde[:], in0=i_tilde[:], in1=a[:], op=ALU.subtract)
             i_p = work.tile([P, BATCH_TILES, BLOCK_ROWS], F32, name="i_p")
             f_p = work.tile([P, BATCH_TILES, BLOCK_ROWS], F32, name="f_p")
-            nc.vector.tensor_scalar_min(out=i_p[:], in0=i_tilde[:], scalar1=0.0)
-            nc.vector.tensor_scalar(
-                out=f_p[:], in0=i_tilde[:], scalar1=-1.0, scalar2=0.0, op0=ALU.mult, op1=ALU.min
-            )
+            halves = [slice(h * ROW_TILES, (h + 1) * ROW_TILES) for h in range(ACT_BLOCKS)]
+            for h in halves:
+                nc.vector.tensor_tensor(out=m_t[:, h, :], in0=a[:, h, :], in1=i_tilde[:, h, :], op=ALU.max)
+            nc.sync.dma_start(out=by_batch(out_0)[:, :, feats], in_=m_t[:])
+            for h in halves:
+                nc.vector.tensor_tensor(
+                    out=i_tilde[:, h, :], in0=i_tilde[:, h, :], in1=a[:, h, :], op=ALU.subtract
+                )
+            for h in halves:
+                nc.vector.tensor_scalar_min(out=i_p[:, h, :], in0=i_tilde[:, h, :], scalar1=0.0)
+            for h in halves:
+                nc.vector.tensor_scalar(
+                    out=f_p[:, h, :], in0=i_tilde[:, h, :], scalar1=-1.0, scalar2=0.0,
+                    op0=ALU.mult, op1=ALU.min,
+                )
             exps[c] = (i_p, f_p)
 
         def exp_stage(c):

@@ -171,24 +171,31 @@ def tile_slstmlayer_pa_kernel(
             pre[u] = out
 
         decay = {}
+        halves = [slice(h * ROW_TILES, (h + 1) * ROW_TILES) for h in range(ACT_BLOCKS)]
 
         def sigmoid(c):
             t = keep.tile([P, BATCH_TILES, BLOCK_ROWS], F32, name="decay_%d" % c)
-            nc.scalar.activation(out=t[:], in_=pre[c][:], func=ACT.Sigmoid)
+            for h in halves:
+                nc.scalar.activation(out=t[:, h, :], in_=pre[c][:, h, :], func=ACT.Sigmoid)
             decay[c] = t
 
         def clamp(c):
             t = decay[c]
-            nc.vector.tensor_scalar_max(out=t[:], in0=t[:], scalar1=SIGMOID_FLOOR)
+            for h in halves:
+                nc.vector.tensor_scalar_max(out=t[:, h, :], in0=t[:, h, :], scalar1=SIGMOID_FLOOR)
 
         def log(c):
             t = decay[c]
-            nc.scalar.activation(out=t[:], in_=t[:], func=ACT.Ln)
+            for h in halves:
+                nc.scalar.activation(out=t[:, h, :], in_=t[:, h, :], func=ACT.Ln)
 
         def add_m_prev(c):
             feats = slice(c * BLOCK_ROWS, (c + 1) * BLOCK_ROWS)
             t = decay[c]
-            nc.vector.tensor_tensor(out=t[:], in0=t[:], in1=m_raw[:, :, feats], op=ALU.add)
+            for h in halves:
+                nc.vector.tensor_tensor(
+                    out=t[:, h, :], in0=t[:, h, :], in1=m_raw[:, h, feats], op=ALU.add
+                )
 
         exps = {}
 
@@ -199,10 +206,10 @@ def tile_slstmlayer_pa_kernel(
             m_t = work.tile([P, BATCH_TILES, BLOCK_ROWS], F32, name="m_t")
             i_p = work.tile([P, BATCH_TILES, BLOCK_ROWS], F32, name="i_p")
             f_p = work.tile([P, BATCH_TILES, BLOCK_ROWS], F32, name="f_p")
-            halves = [slice(h * ROW_TILES, (h + 1) * ROW_TILES) for h in range(ACT_BLOCKS)]
             for h in halves:
                 nc.vector.tensor_tensor(out=m_t[:, h, :], in0=a[:, h, :], in1=i_tilde[:, h, :], op=ALU.max)
-            nc.sync.dma_start(out=by_batch(out_0)[:, :, feats], in_=m_t[:])
+            for h in halves:
+                nc.sync.dma_start(out=by_batch(out_0)[:, h, feats], in_=m_t[:, h, :])
             for h in halves:
                 nc.vector.tensor_tensor(
                     out=i_tilde[:, h, :], in0=i_tilde[:, h, :], in1=a[:, h, :], op=ALU.subtract
@@ -219,8 +226,9 @@ def tile_slstmlayer_pa_kernel(
         def exp_stage(c):
             feats = slice(c * BLOCK_ROWS, (c + 1) * BLOCK_ROWS)
             for t, out in zip(exps[c], (out_1, out_2)):
-                nc.scalar.activation(out=t[:], in_=t[:], func=ACT.Exp)
-                nc.sync.dma_start(out=by_batch(out)[:, :, feats], in_=t[:])
+                for h in halves:
+                    nc.scalar.activation(out=t[:, h, :], in_=t[:, h, :], func=ACT.Exp)
+                    nc.sync.dma_start(out=by_batch(out)[:, h, feats], in_=t[:, h, :])
 
         ctx.enter_context(tc.manual_schedule())
         for k in range(ACT_BLOCKS + 1):

from contextlib import ExitStack

import concourse.mybir as mybir
from concourse.masks import make_identity

F32 = mybir.dt.float32
BF16 = mybir.dt.bfloat16
U32 = mybir.dt.uint32
U8 = mybir.dt.uint8
FP8X4 = mybir.dt.float8_e4m3fn_x4
ACT = mybir.ActivationFunctionType
ALU = mybir.AluOpType

P = 128
BATCH = 512
SIDE_K = 1024
HIDDEN = 1024
K_PASS = 512
SIDES = 2
SIDE_PASSES = SIDE_K // K_PASS
PASSES = SIDES * SIDE_PASSES
BLOCK_ROWS = 256
ROW_TILES = BLOCK_ROWS // P
BATCH_TILES = BATCH // P
CHUNKS = HIDDEN // BLOCK_ROWS
SIDE_WORDS = SIDE_K // 2
WORD_TILES = SIDE_WORDS // P
SIGMOID_FLOOR = 1e-8

FLOPS = 2 * BATCH * (SIDES * SIDE_K) * (2 * HIDDEN)


def tile_slstmlayer_pa_kernel(
    tc, x, h_prev, m_prev, Wi_x, b_i, Wi_h, Wf_x, b_f, Wf_h, out_0, out_1, out_2
):
    nc = tc.nc
    with ExitStack() as ctx:
        const = ctx.enter_context(tc.tile_pool(name="const", bufs=1))
        raw_pool = ctx.enter_context(tc.tile_pool(name="raw", bufs=1))
        grouped_pool = ctx.enter_context(tc.tile_pool(name="grouped", bufs=4))
        act_pool = ctx.enter_context(tc.tile_pool(name="act_codes", bufs=1))
        w_pool = ctx.enter_context(tc.tile_pool(name="w_codes", bufs=3))
        keep = ctx.enter_context(tc.tile_pool(name="keep", bufs=1))
        work = ctx.enter_context(tc.tile_pool(name="work", bufs=3))
        t_psum = ctx.enter_context(tc.psum_pool(name="t_psum", bufs=4))
        acc_psum = ctx.enter_context(tc.psum_pool(name="acc_psum", bufs=4))

        ident = const.tile([P, P], F32, name="ident")
        make_identity(nc, ident[:])

        def by_batch(ap):
            return ap.rearrange("(p t) n -> p t n", t=BATCH_TILES)

        blocks = []
        for pair in range(BATCH_TILES // ROW_TILES):
            tiles = slice(pair * ROW_TILES, (pair + 1) * ROW_TILES)
            blocks.append((by_batch(x)[:, tiles, :], by_batch(h_prev)[:, tiles, :]))
        for w_x, w_h in ((Wf_x, Wf_h), (Wi_x, Wi_h)):
            for c in range(CHUNKS):
                rows = slice(c * BLOCK_ROWS, (c + 1) * BLOCK_ROWS)
                blocks.append(
                    (
                        w_x[rows, :].rearrange("(t p) k -> p t k", p=P),
                        w_h[rows, :].rearrange("(t p) k -> p t k", p=P),
                    )
                )
        ACT_BLOCKS = BATCH_TILES // ROW_TILES
        UNITS = 2 * CHUNKS

        raw = []

        def load_block(k):
            sides = []
            for s in range(SIDES):
                t = raw_pool.tile([P, ROW_TILES * SIDE_K], BF16, name="raw_%d_%d" % (k, s))
                nc.sync.dma_start(
                    out=t[:].rearrange("p (t k) -> p t k", t=ROW_TILES), in_=blocks[k][s]
                )
                sides.append(t)
            raw.append(sides)

        bias_f = const.tile([P, HIDDEN], BF16, name="bias_f")
        bias_i = const.tile([P, HIDDEN], BF16, name="bias_i")
        m_raw = const.tile([P, BATCH_TILES, HIDDEN], BF16, name="m_raw")
        for k in range(ACT_BLOCKS + 2):
            load_block(k)
        nc.sync.dma_start(out=bias_f[:], in_=b_f.partition_broadcast(P))
        for k in range(ACT_BLOCKS + 2, ACT_BLOCKS + CHUNKS + 1):
            load_block(k)
        nc.sync.dma_start(out=m_raw[:], in_=by_batch(m_prev))
        nc.sync.dma_start(out=bias_i[:], in_=b_i.partition_broadcast(P))
        for k in range(ACT_BLOCKS + CHUNKS + 1, ACT_BLOCKS + UNITS):
            load_block(k)

        grouped = {}
        codes = {}
        scales = {}

        def transpose_block(k):
            for s in range(SIDES):
                words = raw[k][s][:].bitcast(F32)
                g = grouped_pool.tile(
                    [P, SIDE_PASSES * BLOCK_ROWS * 4], BF16, name="grouped", align_bytes=64
                )
                g_words = g[:].bitcast(F32).rearrange(
                    "p (g c u) -> p g c u", g=SIDE_PASSES, u=2
                )
                for t in range(ROW_TILES):
                    bank = t_psum.tile([P, WORD_TILES, P], F32, name="bank")
                    for j in range(WORD_TILES):
                        first = t * SIDE_WORDS + j * P
                        nc.tensor.transpose(bank[:, j, :], words[:, first : first + P], ident[:])
                    nc.scalar.copy(
                        out=g_words[:, :, t * P : (t + 1) * P, :],
                        in_=bank[:].rearrange("p (g u) r -> p g r u", u=2),
                    )
                grouped[(k, s)] = g

        def quantise_block(k):
            pool = act_pool if k < ACT_BLOCKS else w_pool
            tag = "act_%d" % k if k < ACT_BLOCKS else "w"
            cd = pool.tile(
                [P, PASSES * BLOCK_ROWS], U32, name="codes_" + tag, align_bytes=64
            )
            sc = pool.tile(
                [P, PASSES * BLOCK_ROWS], U8, name="scales_" + tag, align_bytes=64
            )
            for s in range(SIDES):
                cols = slice(s * SIDE_PASSES * BLOCK_ROWS, (s + 1) * SIDE_PASSES * BLOCK_ROWS)
                nc.vector.quantize_mx(
                    out=cd[:, cols].bitcast(FP8X4), scales=sc[:, cols], in_=grouped[(k, s)][:]
                )
            codes[k] = cd
            scales[k] = sc

        acc = {}

        def multiply(u):
            k = ACT_BLOCKS + u
            for pair in range(ACT_BLOCKS):
                bank = acc_psum.tile([P, ROW_TILES, BLOCK_ROWS], F32, name="acc")
                for t in range(ROW_TILES):
                    for q in range(PASSES):
                        a_cols = slice(q * BLOCK_ROWS + t * P, q * BLOCK_ROWS + (t + 1) * P)
                        w_cols = slice(q * BLOCK_ROWS, (q + 1) * BLOCK_ROWS)
                        nc.tensor.matmul_mx(
                            out=bank[:, t, :],
                            lhsT=codes[pair][:, a_cols].bitcast(FP8X4),
                            lhsT_scale=scales[pair][:, a_cols],
                            rhs=codes[k][:, w_cols].bitcast(FP8X4),
                            rhs_scale=scales[k][:, w_cols],
                            start=(q == 0),
                            stop=(q == PASSES - 1),
                        )
                acc[(u, pair)] = bank

        pre = {}

        def add_bias(u):
            bias = bias_f if u < CHUNKS else bias_i
            c = u % CHUNKS
            feats = slice(c * BLOCK_ROWS, (c + 1) * BLOCK_ROWS)
            out = work.tile([P, BATCH_TILES, BLOCK_ROWS], F32, name="pre")
            for pair in range(ACT_BLOCKS):
                nc.vector.tensor_tensor(
                    out=out[:, pair * ROW_TILES : (pair + 1) * ROW_TILES, :],
                    in0=acc[(u, pair)][:],
                    in1=bias[:, feats].unsqueeze(1).to_broadcast([P, ROW_TILES, BLOCK_ROWS]),
                    op=ALU.add,
                )
            pre[u] = out

        decay = {}
        halves = [slice(h * ROW_TILES, (h + 1) * ROW_TILES) for h in range(ACT_BLOCKS)]

        def sigmoid(c):
            t = keep.tile([P, BATCH_TILES, BLOCK_ROWS], F32, name="decay_%d" % c)
            for h in halves:
                nc.scalar.activation(out=t[:, h, :], in_=pre[c][:, h, :], func=ACT.Sigmoid)
            decay[c] = t

        def clamp(c):
            t = decay[c]
            for h in halves:
                nc.vector.tensor_scalar_max(out=t[:, h, :], in0=t[:, h, :], scalar1=SIGMOID_FLOOR)

        def log(c):
            t = decay[c]
            for h in halves:
                nc.scalar.activation(out=t[:, h, :], in_=t[:, h, :], func=ACT.Ln)

        def add_m_prev(c):
            feats = slice(c * BLOCK_ROWS, (c + 1) * BLOCK_ROWS)
            t = decay[c]
            for h in halves:
                nc.vector.tensor_tensor(
                    out=t[:, h, :], in0=t[:, h, :], in1=m_raw[:, h, feats], op=ALU.add
                )

        exps = {}

        def stabilise_stage(c):
            feats = slice(c * BLOCK_ROWS, (c + 1) * BLOCK_ROWS)
            i_tilde = pre[CHUNKS + c]
            a = decay[c]
            m_t = work.tile([P, BATCH_TILES, BLOCK_ROWS], F32, name="m_t")
            i_p = work.tile([P, BATCH_TILES, BLOCK_ROWS], F32, name="i_p")
            f_p = work.tile([P, BATCH_TILES, BLOCK_ROWS], F32, name="f_p")
            for h in halves:
                nc.vector.tensor_tensor(out=m_t[:, h, :], in0=a[:, h, :], in1=i_tilde[:, h, :], op=ALU.max)
            for h in halves:
                nc.sync.dma_start(out=by_batch(out_0)[:, h, feats], in_=m_t[:, h, :])
            for h in halves:
                nc.vector.tensor_tensor(
                    out=i_tilde[:, h, :], in0=i_tilde[:, h, :], in1=a[:, h, :], op=ALU.subtract
                )
            for h in halves:
                nc.vector.tensor_scalar_min(out=i_p[:, h, :], in0=i_tilde[:, h, :], scalar1=0.0)
            for h in halves:
                nc.vector.tensor_scalar(
                    out=f_p[:, h, :], in0=i_tilde[:, h, :], scalar1=-1.0, scalar2=0.0,
                    op0=ALU.mult, op1=ALU.min,
                )
            exps[c] = (i_p, f_p)

        def exp_stage(c):
            feats = slice(c * BLOCK_ROWS, (c + 1) * BLOCK_ROWS)
            for t, out in zip(exps[c], (out_1, out_2)):
                for h in halves:
                    nc.scalar.activation(out=t[:, h, :], in_=t[:, h, :], func=ACT.Exp)
                    nc.sync.dma_start(out=by_batch(out)[:, h, feats], in_=t[:, h, :])

        ctx.enter_context(tc.manual_schedule())
        for k in range(ACT_BLOCKS + 1):
            transpose_block(k)
            quantise_block(k)
        for u in range(UNITS + 2):
            logs = [2 * (u - CHUNKS - 1) + i for i in range(2)] if u in (CHUNKS + 1, CHUNKS + 2) else []
            for c in logs:
                log(c)
            if u + 1 < UNITS:
                transpose_block(ACT_BLOCKS + u + 1)
            if u < UNITS:
                multiply(u)
            if 1 <= u <= UNITS:
                add_bias(u - 1)
            if 2 <= u <= CHUNKS + 1:
                clamp(u - 2)
            for c in logs:
                add_m_prev(c)
            if u + 1 < UNITS:
                quantise_block(ACT_BLOCKS + u + 1)
            if 1 <= u <= CHUNKS:
                sigmoid(u - 1)
            if CHUNKS + 1 <= u <= UNITS:
                stabilise_stage(u - 1 - CHUNKS)
            if CHUNKS + 2 <= u:
                exp_stage(u - 2 - CHUNKS)
